import numpy as np
import ml_dtypes

BF16 = ml_dtypes.bfloat16


def bf(x):
    return np.asarray(x, np.float32).astype(BF16)


def f32(x):
    return np.asarray(x, np.float32)


def f64(x):
    return np.asarray(x).astype(np.float64)


def striped(idx):
    return np.tile(idx.reshape(-1, 16).T, (8, 1))


C, K, H, S, N, P = 256, 2, 128, 1024, 128, 256
HALF = H // 2
THETA = 5000000.0
AXES, SEC_H, SEC_W = 3, 20, 20


def rope_tables():
    pos = np.stack([np.flatnonzero(np.random.permutation(P) < N) for _ in range(AXES)])
    inv = THETA ** (-np.arange(HALF) / HALF)
    which = np.zeros(HALF, np.int64)
    which[1:SEC_H * AXES:AXES] = 1
    which[2:SEC_W * AXES:AXES] = 2
    ang = pos[which] * inv[:, None]
    emb = np.concatenate([ang, ang], axis=0)
    return np.cos(emb), np.sin(emb)


def setup_inputs():
    z = np.random.standard_normal((K, H, N))
    kn = z / np.sqrt(np.mean(z * z, axis=1, keepdims=True))
    ct, st = rope_tables()
    return {"base": f32(np.random.standard_normal((C, S))), "kn": f32(kn.reshape(C, N)), "gain": f32(1.0 + 0.1 * np.random.standard_normal((H, 1))), "cos_tab": f32(ct), "sin_tab": f32(st), "offs": striped(np.random.permutation(S)[:N])}


def reference(base, kn, gain, cos_tab, sin_tab, offs):
    idx = offs[:16].T.reshape(-1)
    ks = f64(gain)[None] * f64(kn).reshape(K, H, N)
    rot = np.concatenate([-ks[:, HALF:], ks[:, :HALF]], axis=1)
    new = ks * f64(cos_tab)[None] + rot * f64(sin_tab)[None]
    out = f64(base).copy()
    out[:, idx] = new.reshape(C, N)
    return out

@@ -1,0 +1,57 @@
+import concourse.mybir as mybir
+
+F32 = mybir.dt.float32
+U16 = mybir.dt.uint16
+MULT = mybir.AluOpType.mult
+ADD = mybir.AluOpType.add
+
+HEADS = 2
+FEATURES = 128
+HALF = FEATURES // 2
+TOKENS = 128
+SLOTS = 1024
+
+
+def tile_qwen3vltextattention_kernel(tc, base, kn, gain, cos_tab, sin_tab, offs, out):
+    nc = tc.nc
+    kn_by_feature = kn.rearrange("(a h) j -> h a j", a=HEADS)
+
+    with tc.tile_pool(name="held", bufs=1) as held:
+        offsets = held.tile([FEATURES, TOKENS // 16], U16, name="offsets")
+        nc.sync.dma_start(offsets[:], offs)
+
+        windows = []
+        for a in range(HEADS):
+            window = held.tile([FEATURES, SLOTS], F32, name=f"window{a}")
+            nc.sync.dma_start(window[:], base[a * FEATURES : (a + 1) * FEATURES, :])
+            windows.append(window)
+
+        keys = held.tile([FEATURES, HEADS, TOKENS], F32, name="keys")
+        partner_keys = held.tile([FEATURES, HEADS, TOKENS], F32, name="partner_keys")
+        nc.scalar.dma_start(keys[:], kn_by_feature)
+        nc.scalar.dma_start(partner_keys[0:HALF], kn_by_feature[HALF:FEATURES])
+        nc.scalar.dma_start(partner_keys[HALF:FEATURES], kn_by_feature[0:HALF])
+
+        cosines = held.tile([FEATURES, TOKENS], F32, name="cosines")
+        sines = held.tile([FEATURES, TOKENS], F32, name="sines")
+        nc.scalar.dma_start(cosines[:], cos_tab)
+        nc.scalar.dma_start(sines[:], sin_tab)
+
+        own_gain = held.tile([FEATURES, 1], F32, name="own_gain")
+        partner_gain = held.tile([FEATURES, 1], F32, name="partner_gain")
+        nc.gpsimd.dma_start(own_gain[:], gain)
+        nc.gpsimd.dma_start(partner_gain[0:HALF], gain[HALF:FEATURES])
+        nc.gpsimd.dma_start(partner_gain[HALF:FEATURES], gain[0:HALF])
+        nc.vector.tensor_scalar_mul(partner_gain[0:HALF], partner_gain[0:HALF], -1.0)
+
+        for a in range(HEADS):
+            direct = held.tile([FEATURES, TOKENS], F32, name=f"direct{a}")
+            rotated = held.tile([FEATURES, TOKENS], F32, name=f"rotated{a}")
+            nc.vector.scalar_tensor_tensor(
+                direct[:], keys[:, a, :], own_gain[:, 0:1], cosines[:], MULT, MULT
+            )
+            nc.vector.scalar_tensor_tensor(
+                rotated[:], partner_keys[:, a, :], partner_gain[:, 0:1], sines[:], MULT, MULT
+            )
+            nc.vector.tensor_tensor(windows[a][:].indirect(offsets[:]), direct[:], rotated[:], ADD)
+            nc.sync.dma_start(out[a * FEATURES : (a + 1) * FEATURES, :], windows[a][:])

@@ -1,4 +1,5 @@
 import concourse.mybir as mybir
+from concourse.masks import make_identity
 
 F32 = mybir.dt.float32
 U16 = mybir.dt.uint16
@@ -14,11 +15,21 @@ SLOTS = 1024
 
 def tile_qwen3vltextattention_kernel(tc, base, kn, gain, cos_tab, sin_tab, offs, out):
     nc = tc.nc
-    kn_by_feature = kn.rearrange("(a h) j -> h a j", a=HEADS)
 
-    with tc.tile_pool(name="held", bufs=1) as held:
+    with (
+        tc.tile_pool(name="held", bufs=1) as held,
+        tc.psum_pool(name="psum", bufs=1) as psum,
+    ):
         offsets = held.tile([FEATURES, TOKENS // 16], U16, name="offsets")
         nc.sync.dma_start(offsets[:], offs)
+        gains = held.tile([FEATURES, 1], F32, name="gains")
+        nc.sync.dma_start(gains[:], gain)
+        keys = held.tile([FEATURES, HEADS, TOKENS], F32, name="keys")
+        nc.sync.dma_start(keys[:], kn.rearrange("(a h) j -> h a j", a=HEADS))
+        cosines = held.tile([FEATURES, TOKENS], F32, name="cosines")
+        nc.sync.dma_start(cosines[:], cos_tab)
+        sines = held.tile([FEATURES, TOKENS], F32, name="sines")
+        nc.sync.dma_start(sines[:], sin_tab)
 
         windows = []
         for a in range(HEADS):
@@ -26,32 +37,26 @@ def tile_qwen3vltextattention_kernel(tc, base, kn, gain, cos_tab, sin_tab, offs,
             nc.sync.dma_start(window[:], base[a * FEATURES : (a + 1) * FEATURES, :])
             windows.append(window)
 
-        keys = held.tile([FEATURES, HEADS, TOKENS], F32, name="keys")
-        partner_keys = held.tile([FEATURES, HEADS, TOKENS], F32, name="partner_keys")
-        nc.scalar.dma_start(keys[:], kn_by_feature)
-        nc.scalar.dma_start(partner_keys[0:HALF], kn_by_feature[HALF:FEATURES])
-        nc.scalar.dma_start(partner_keys[HALF:FEATURES], kn_by_feature[0:HALF])
+        identity = held.tile([FEATURES, FEATURES], F32, name="identity")
+        make_identity(nc, identity[:])
+        rotate = held.tile([FEATURES, FEATURES], F32, name="rotate")
+        nc.vector.tensor_scalar(
+            rotate[:, 0:HALF], identity[:, HALF:FEATURES], gains[:, 0:1], -1.0, MULT, MULT
+        )
+        nc.vector.tensor_scalar_mul(rotate[:, HALF:FEATURES], identity[:, 0:HALF], gains[:, 0:1])
 
-        cosines = held.tile([FEATURES, TOKENS], F32, name="cosines")
-        sines = held.tile([FEATURES, TOKENS], F32, name="sines")
-        nc.scalar.dma_start(cosines[:], cos_tab)
-        nc.scalar.dma_start(sines[:], sin_tab)
-
-        own_gain = held.tile([FEATURES, 1], F32, name="own_gain")
-        partner_gain = held.tile([FEATURES, 1], F32, name="partner_gain")
-        nc.gpsimd.dma_start(own_gain[:], gain)
-        nc.gpsimd.dma_start(partner_gain[0:HALF], gain[HALF:FEATURES])
-        nc.gpsimd.dma_start(partner_gain[HALF:FEATURES], gain[0:HALF])
-        nc.vector.tensor_scalar_mul(partner_gain[0:HALF], partner_gain[0:HALF], -1.0)
+        direct = held.tile([FEATURES, HEADS, TOKENS], F32, name="direct")
+        rotated = held.tile([FEATURES, HEADS, TOKENS], F32, name="rotated")
+        for a in range(HEADS):
+            rot = psum.tile([FEATURES, TOKENS], F32, name=f"rot{a}")
+            nc.tensor.matmul(rot[:], rotate[:], keys[:, a, :])
+            nc.vector.scalar_tensor_tensor(
+                direct[:, a, :], keys[:, a, :], gains[:, 0:1], cosines[:], MULT, MULT
+            )
+            nc.vector.tensor_tensor(rotated[:, a, :], rot[:], sines[:], MULT)
 
         for a in range(HEADS):
-            direct = held.tile([FEATURES, TOKENS], F32, name=f"direct{a}")
-            rotated = held.tile([FEATURES, TOKENS], F32, name=f"rotated{a}")
-            nc.vector.scalar_tensor_tensor(
-                direct[:], keys[:, a, :], own_gain[:, 0:1], cosines[:], MULT, MULT
+            nc.vector.tensor_tensor(
+                windows[a][:].indirect(offsets[:]), direct[:, a, :], rotated[:, a, :], ADD
             )
-            nc.vector.scalar_tensor_tensor(
-                rotated[:], partner_keys[:, a, :], partner_gain[:, 0:1], sines[:], MULT, MULT
-            )
-            nc.vector.tensor_tensor(windows[a][:].indirect(offsets[:]), direct[:], rotated[:], ADD)
             nc.sync.dma_start(out[a * FEATURES : (a + 1) * FEATURES, :], windows[a][:])

@@ -1,10 +1,10 @@
 import concourse.mybir as mybir
-from concourse.masks import make_identity
 
 F32 = mybir.dt.float32
 U16 = mybir.dt.uint16
 MULT = mybir.AluOpType.mult
 ADD = mybir.AluOpType.add
+NOT_EQUAL = mybir.AluOpType.not_equal
 
 HEADS = 2
 FEATURES = 128
@@ -37,25 +37,32 @@ def tile_qwen3vltextattention_kernel(tc, base, kn, gain, cos_tab, sin_tab, offs,
             nc.sync.dma_start(window[:], base[a * FEATURES : (a + 1) * FEATURES, :])
             windows.append(window)
 
-        identity = held.tile([FEATURES, FEATURES], F32, name="identity")
-        make_identity(nc, identity[:])
-        rotate = held.tile([FEATURES, FEATURES], F32, name="rotate")
-        nc.vector.tensor_scalar(
-            rotate[:, 0:HALF], identity[:, HALF:FEATURES], gains[:, 0:1], -1.0, MULT, MULT
-        )
-        nc.vector.tensor_scalar_mul(rotate[:, HALF:FEATURES], identity[:, 0:HALF], gains[:, 0:1])
+        swap = held.tile([FEATURES, FEATURES], F32, name="swap")
+        nc.gpsimd.memset(swap[:], 0.0)
+        for sign in (-1.0, 1.0):
+            nc.gpsimd.affine_select(
+                out=swap[:],
+                in_=swap[:],
+                pattern=[[-1, FEATURES]],
+                compare_op=NOT_EQUAL,
+                fill=sign,
+                base=int(sign) * HALF,
+                channel_multiplier=1,
+            )
 
+        scaled = held.tile([FEATURES, HEADS, TOKENS], F32, name="scaled")
         direct = held.tile([FEATURES, HEADS, TOKENS], F32, name="direct")
         rotated = held.tile([FEATURES, HEADS, TOKENS], F32, name="rotated")
+        rots = []
         for a in range(HEADS):
+            nc.vector.tensor_scalar_mul(scaled[:, a, :], keys[:, a, :], gains[:, 0:1])
             rot = psum.tile([FEATURES, TOKENS], F32, name=f"rot{a}")
-            nc.tensor.matmul(rot[:], rotate[:], keys[:, a, :])
-            nc.vector.scalar_tensor_tensor(
-                direct[:, a, :], keys[:, a, :], gains[:, 0:1], cosines[:], MULT, MULT
-            )
-            nc.vector.tensor_tensor(rotated[:, a, :], rot[:], sines[:], MULT)
+            nc.tensor.matmul(rot[:], swap[:], scaled[:, a, :])
+            rots.append(rot)
+            nc.vector.tensor_tensor(direct[:, a, :], scaled[:, a, :], cosines[:], MULT)
 
         for a in range(HEADS):
+            nc.vector.tensor_tensor(rotated[:, a, :], rots[a][:], sines[:], MULT)
             nc.vector.tensor_tensor(
                 windows[a][:].indirect(offsets[:]), direct[:, a, :], rotated[:, a, :], ADD
             )

@@ -20,16 +20,16 @@ def tile_qwen3vltextattention_kernel(tc, base, kn, gain, cos_tab, sin_tab, offs,
         tc.tile_pool(name="held", bufs=1) as held,
         tc.psum_pool(name="psum", bufs=1) as psum,
     ):
-        offsets = held.tile([FEATURES, TOKENS // 16], U16, name="offsets")
-        nc.sync.dma_start(offsets[:], offs)
         gains = held.tile([FEATURES, 1], F32, name="gains")
         nc.sync.dma_start(gains[:], gain)
         keys = held.tile([FEATURES, HEADS, TOKENS], F32, name="keys")
         nc.sync.dma_start(keys[:], kn.rearrange("(a h) j -> h a j", a=HEADS))
         cosines = held.tile([FEATURES, TOKENS], F32, name="cosines")
-        nc.sync.dma_start(cosines[:], cos_tab)
+        nc.scalar.dma_start(cosines[:], cos_tab)
         sines = held.tile([FEATURES, TOKENS], F32, name="sines")
-        nc.sync.dma_start(sines[:], sin_tab)
+        nc.scalar.dma_start(sines[:], sin_tab)
+        offsets = held.tile([FEATURES, TOKENS // 16], U16, name="offsets")
+        nc.sync.dma_start(offsets[:], offs)
 
         windows = []
         for a in range(HEADS):

@@ -20,16 +20,16 @@ def tile_qwen3vltextattention_kernel(tc, base, kn, gain, cos_tab, sin_tab, offs,
         tc.tile_pool(name="held", bufs=1) as held,
         tc.psum_pool(name="psum", bufs=1) as psum,
     ):
+        offsets = held.tile([FEATURES, TOKENS // 16], U16, name="offsets")
+        nc.sync.dma_start(offsets[:], offs)
         gains = held.tile([FEATURES, 1], F32, name="gains")
         nc.sync.dma_start(gains[:], gain)
         keys = held.tile([FEATURES, HEADS, TOKENS], F32, name="keys")
         nc.sync.dma_start(keys[:], kn.rearrange("(a h) j -> h a j", a=HEADS))
         cosines = held.tile([FEATURES, TOKENS], F32, name="cosines")
-        nc.scalar.dma_start(cosines[:], cos_tab)
+        nc.sync.dma_start(cosines[:], cos_tab)
         sines = held.tile([FEATURES, TOKENS], F32, name="sines")
-        nc.scalar.dma_start(sines[:], sin_tab)
-        offsets = held.tile([FEATURES, TOKENS // 16], U16, name="offsets")
-        nc.sync.dma_start(offsets[:], offs)
+        nc.sync.dma_start(sines[:], sin_tab)
 
         windows = []
         for a in range(HEADS):
@@ -38,15 +38,16 @@ def tile_qwen3vltextattention_kernel(tc, base, kn, gain, cos_tab, sin_tab, offs,
             windows.append(window)
 
         swap = held.tile([FEATURES, FEATURES], F32, name="swap")
-        nc.gpsimd.memset(swap[:], 0.0)
-        for sign in (-1.0, 1.0):
+        nc.vector.memset(swap[:], 0.0)
+        for first_column, fill, base in ((0, -1.0, -HALF), (HALF, 1.0, 0)):
+            half = swap[:, first_column : first_column + HALF]
             nc.gpsimd.affine_select(
-                out=swap[:],
-                in_=swap[:],
-                pattern=[[-1, FEATURES]],
+                out=half,
+                in_=half,
+                pattern=[[-1, HALF]],
                 compare_op=NOT_EQUAL,
-                fill=sign,
-                base=int(sign) * HALF,
+                fill=fill,
+                base=base,
                 channel_multiplier=1,
             )
 

@@ -22,8 +22,13 @@ def tile_qwen3vltextattention_kernel(tc, base, kn, gain, cos_tab, sin_tab, offs,
     ):
         offsets = held.tile([FEATURES, TOKENS // 16], U16, name="offsets")
         nc.sync.dma_start(offsets[:], offs)
-        gains = held.tile([FEATURES, 1], F32, name="gains")
-        nc.sync.dma_start(gains[:], gain)
+        gain_pairs = held.tile([FEATURES, 2], F32, name="gain_pairs")
+        with nc.allow_non_contiguous_dma(reason="128 single gains to a load"):
+            for half in range(2):
+                nc.sync.dma_start(
+                    gain_pairs[half * HALF : (half + 1) * HALF, :],
+                    gain.rearrange("(s q) o -> q (s o)", s=2),
+                )
         keys = held.tile([FEATURES, HEADS, TOKENS], F32, name="keys")
         nc.sync.dma_start(keys[:], kn.rearrange("(a h) j -> h a j", a=HEADS))
         cosines = held.tile([FEATURES, TOKENS], F32, name="cosines")
@@ -38,32 +43,42 @@ def tile_qwen3vltextattention_kernel(tc, base, kn, gain, cos_tab, sin_tab, offs,
             windows.append(window)
 
         swap = held.tile([FEATURES, FEATURES], F32, name="swap")
-        nc.vector.memset(swap[:], 0.0)
-        for first_column, fill, base in ((0, -1.0, -HALF), (HALF, 1.0, 0)):
-            half = swap[:, first_column : first_column + HALF]
+        nc.gpsimd.memset(swap[:], 0.0)
+        for shift in (-HALF, HALF):
             nc.gpsimd.affine_select(
-                out=half,
-                in_=half,
-                pattern=[[-1, HALF]],
+                out=swap[:],
+                in_=swap[:],
+                pattern=[[-1, FEATURES]],
                 compare_op=NOT_EQUAL,
-                fill=fill,
-                base=base,
+                fill=1.0,
+                base=shift,
                 channel_multiplier=1,
             )
+        partners = []
+        for a in range(HEADS):
+            partner = psum.tile([FEATURES, TOKENS], F32, name=f"partner{a}")
+            nc.tensor.matmul(partner[:], swap[:], keys[:, a, :])
+            partners.append(partner)
 
-        scaled = held.tile([FEATURES, HEADS, TOKENS], F32, name="scaled")
+        gained_cos = held.tile([FEATURES, TOKENS], F32, name="gained_cos")
+        gained_sin = held.tile([FEATURES, TOKENS], F32, name="gained_sin")
+        for half, sign in ((0, -1.0), (1, 1.0)):
+            rows = slice(half * HALF, (half + 1) * HALF)
+            nc.vector.tensor_scalar_mul(
+                gained_cos[rows, :], cosines[rows, :], gain_pairs[rows, half : half + 1]
+            )
+            nc.vector.tensor_scalar(
+                gained_sin[rows, :], sines[rows, :], gain_pairs[rows, 1 - half : 2 - half], sign,
+                MULT, MULT,
+            )
+
         direct = held.tile([FEATURES, HEADS, TOKENS], F32, name="direct")
         rotated = held.tile([FEATURES, HEADS, TOKENS], F32, name="rotated")
-        rots = []
         for a in range(HEADS):
-            nc.vector.tensor_scalar_mul(scaled[:, a, :], keys[:, a, :], gains[:, 0:1])
-            rot = psum.tile([FEATURES, TOKENS], F32, name=f"rot{a}")
-            nc.tensor.matmul(rot[:], swap[:], scaled[:, a, :])
-            rots.append(rot)
-            nc.vector.tensor_tensor(direct[:, a, :], scaled[:, a, :], cosines[:], MULT)
+            nc.vector.tensor_tensor(direct[:, a, :], keys[:, a, :], gained_cos[:], MULT)
 
         for a in range(HEADS):
-            nc.vector.tensor_tensor(rotated[:, a, :], rots[a][:], sines[:], MULT)
+            nc.vector.tensor_tensor(rotated[:, a, :], partners[a][:], gained_sin[:], MULT)
             nc.vector.tensor_tensor(
                 windows[a][:].indirect(offsets[:]), direct[:, a, :], rotated[:, a, :], ADD
             )

@@ -20,66 +20,70 @@ def tile_qwen3vltextattention_kernel(tc, base, kn, gain, cos_tab, sin_tab, offs,
         tc.tile_pool(name="held", bufs=1) as held,
         tc.psum_pool(name="psum", bufs=1) as psum,
     ):
-        offsets = held.tile([FEATURES, TOKENS // 16], U16, name="offsets")
-        nc.sync.dma_start(offsets[:], offs)
-        gain_pairs = held.tile([FEATURES, 2], F32, name="gain_pairs")
-        with nc.allow_non_contiguous_dma(reason="128 single gains to a load"):
-            for half in range(2):
-                nc.sync.dma_start(
-                    gain_pairs[half * HALF : (half + 1) * HALF, :],
-                    gain.rearrange("(s q) o -> q (s o)", s=2),
-                )
-        keys = held.tile([FEATURES, HEADS, TOKENS], F32, name="keys")
-        nc.sync.dma_start(keys[:], kn.rearrange("(a h) j -> h a j", a=HEADS))
+
+        gain_row = held.tile([1, 2 * FEATURES], F32, name="gain_row")
+        nc.sync.dma_start(
+            gain_row[:].rearrange("p (r h) -> p r h", r=2),
+            gain.rearrange("h o -> o h").unsqueeze(1).to_broadcast([1, 2, FEATURES]),
+        )
+        blocks = [slice(a * FEATURES, (a + 1) * FEATURES) for a in range(HEADS)]
+        keys = []
+        for a in range(HEADS):
+            head_keys = held.tile([FEATURES, TOKENS], F32, name=f"keys{a}")
+            nc.sync.dma_start(head_keys[:], kn[blocks[a], :])
+            keys.append(head_keys)
         cosines = held.tile([FEATURES, TOKENS], F32, name="cosines")
         nc.sync.dma_start(cosines[:], cos_tab)
         sines = held.tile([FEATURES, TOKENS], F32, name="sines")
         nc.sync.dma_start(sines[:], sin_tab)
-
+        offsets = held.tile([FEATURES, TOKENS // 16], U16, name="offsets")
+        nc.sync.dma_start(offsets[:], offs)
         windows = []
         for a in range(HEADS):
             window = held.tile([FEATURES, SLOTS], F32, name=f"window{a}")
-            nc.sync.dma_start(window[:], base[a * FEATURES : (a + 1) * FEATURES, :])
+            nc.sync.dma_start(window[:], base[blocks[a], :])
             windows.append(window)
+
+        one = held.tile([1, 1], F32, name="one")
+        nc.vector.memset(one[:], 1.0)
+        gain_columns = psum.tile([FEATURES, 2], F32, name="gain_columns")
+        own_gain, partner_gain = gain_columns[:, 0:1], gain_columns[:, 1:2]
+        nc.tensor.matmul(own_gain, gain_row[:, 0:FEATURES], one[:])
+        nc.tensor.matmul(partner_gain, gain_row[:, HALF : HALF + FEATURES], one[:])
 
         swap = held.tile([FEATURES, FEATURES], F32, name="swap")
         nc.gpsimd.memset(swap[:], 0.0)
-        for shift in (-HALF, HALF):
+        for sign in (-1.0, 1.0):
             nc.gpsimd.affine_select(
                 out=swap[:],
                 in_=swap[:],
                 pattern=[[-1, FEATURES]],
                 compare_op=NOT_EQUAL,
-                fill=1.0,
-                base=shift,
+                fill=sign,
+                base=int(sign) * HALF,
                 channel_multiplier=1,
             )
         partners = []
         for a in range(HEADS):
             partner = psum.tile([FEATURES, TOKENS], F32, name=f"partner{a}")
-            nc.tensor.matmul(partner[:], swap[:], keys[:, a, :])
+            nc.tensor.matmul(partner[:], swap[:], keys[a][:])
             partners.append(partner)
 
         gained_cos = held.tile([FEATURES, TOKENS], F32, name="gained_cos")
         gained_sin = held.tile([FEATURES, TOKENS], F32, name="gained_sin")
-        for half, sign in ((0, -1.0), (1, 1.0)):
-            rows = slice(half * HALF, (half + 1) * HALF)
-            nc.vector.tensor_scalar_mul(
-                gained_cos[rows, :], cosines[rows, :], gain_pairs[rows, half : half + 1]
-            )
-            nc.vector.tensor_scalar(
-                gained_sin[rows, :], sines[rows, :], gain_pairs[rows, 1 - half : 2 - half], sign,
-                MULT, MULT,
-            )
+        nc.vector.tensor_scalar_mul(gained_cos[:], cosines[:], own_gain)
+        nc.vector.tensor_scalar_mul(gained_sin[:], sines[:], partner_gain)
 
-        direct = held.tile([FEATURES, HEADS, TOKENS], F32, name="direct")
-        rotated = held.tile([FEATURES, HEADS, TOKENS], F32, name="rotated")
+        directs = []
         for a in range(HEADS):
-            nc.vector.tensor_tensor(direct[:, a, :], keys[:, a, :], gained_cos[:], MULT)
+            direct = held.tile([FEATURES, TOKENS], F32, name=f"direct{a}")
+            nc.vector.tensor_tensor(direct[:], keys[a][:], gained_cos[:], MULT)
+            directs.append(direct)
 
         for a in range(HEADS):
-            nc.vector.tensor_tensor(rotated[:, a, :], partners[a][:], gained_sin[:], MULT)
+            rotated = held.tile([FEATURES, TOKENS], F32, name=f"rotated{a}")
+            nc.vector.tensor_tensor(rotated[:], partners[a][:], gained_sin[:], MULT)
             nc.vector.tensor_tensor(
-                windows[a][:].indirect(offsets[:]), direct[:, a, :], rotated[:, a, :], ADD
+                windows[a][:].indirect(offsets[:]), directs[a][:], rotated[:], ADD
             )
-            nc.sync.dma_start(out[a * FEATURES : (a + 1) * FEATURES, :], windows[a][:])
+            nc.sync.dma_start(out[blocks[a], :], windows[a][:])

@@ -69,20 +69,17 @@ def tile_qwen3vltextattention_kernel(tc, base, kn, gain, cos_tab, sin_tab, offs,
             nc.tensor.matmul(partner[:], swap[:], keys[a][:])
             partners.append(partner)
 
-        gained_cos = held.tile([FEATURES, TOKENS], F32, name="gained_cos")
-        gained_sin = held.tile([FEATURES, TOKENS], F32, name="gained_sin")
-        nc.vector.tensor_scalar_mul(gained_cos[:], cosines[:], own_gain)
-        nc.vector.tensor_scalar_mul(gained_sin[:], sines[:], partner_gain)
-
         directs = []
         for a in range(HEADS):
             direct = held.tile([FEATURES, TOKENS], F32, name=f"direct{a}")
-            nc.vector.tensor_tensor(direct[:], keys[a][:], gained_cos[:], MULT)
+            nc.vector.scalar_tensor_tensor(direct[:], keys[a][:], own_gain, cosines[:], MULT, MULT)
             directs.append(direct)
 
         for a in range(HEADS):
             rotated = held.tile([FEATURES, TOKENS], F32, name=f"rotated{a}")
-            nc.vector.tensor_tensor(rotated[:], partners[a][:], gained_sin[:], MULT)
+            nc.vector.scalar_tensor_tensor(
+                rotated[:], partners[a][:], partner_gain, sines[:], MULT, MULT
+            )
             nc.vector.tensor_tensor(
                 windows[a][:].indirect(offsets[:]), directs[a][:], rotated[:], ADD
             )

@@ -22,16 +22,14 @@ def tile_qwen3vltextattention_kernel(tc, base, kn, gain, cos_tab, sin_tab, offs,
     ):
 
         gain_row = held.tile([1, 2 * FEATURES], F32, name="gain_row")
-        nc.sync.dma_start(
+        nc.scalar.dma_start(
             gain_row[:].rearrange("p (r h) -> p r h", r=2),
             gain.rearrange("h o -> o h").unsqueeze(1).to_broadcast([1, 2, FEATURES]),
         )
         blocks = [slice(a * FEATURES, (a + 1) * FEATURES) for a in range(HEADS)]
-        keys = []
-        for a in range(HEADS):
-            head_keys = held.tile([FEATURES, TOKENS], F32, name=f"keys{a}")
-            nc.sync.dma_start(head_keys[:], kn[blocks[a], :])
-            keys.append(head_keys)
+        both_keys = held.tile([FEATURES, HEADS, TOKENS], F32, name="both_keys")
+        nc.sync.dma_start(both_keys[:], kn.rearrange("(a h) j -> h a j", a=HEADS))
+        keys = [both_keys[:, a, :] for a in range(HEADS)]
         cosines = held.tile([FEATURES, TOKENS], F32, name="cosines")
         nc.sync.dma_start(cosines[:], cos_tab)
         sines = held.tile([FEATURES, TOKENS], F32, name="sines")
@@ -66,13 +64,13 @@ def tile_qwen3vltextattention_kernel(tc, base, kn, gain, cos_tab, sin_tab, offs,
         partners = []
         for a in range(HEADS):
             partner = psum.tile([FEATURES, TOKENS], F32, name=f"partner{a}")
-            nc.tensor.matmul(partner[:], swap[:], keys[a][:])
+            nc.tensor.matmul(partner[:], swap[:], keys[a])
             partners.append(partner)
 
         directs = []
         for a in range(HEADS):
             direct = held.tile([FEATURES, TOKENS], F32, name=f"direct{a}")
-            nc.vector.scalar_tensor_tensor(direct[:], keys[a][:], own_gain, cosines[:], MULT, MULT)
+            nc.vector.scalar_tensor_tensor(direct[:], keys[a], own_gain, cosines[:], MULT, MULT)
             directs.append(direct)
 
         for a in range(HEADS):

@@ -22,7 +22,7 @@ def tile_qwen3vltextattention_kernel(tc, base, kn, gain, cos_tab, sin_tab, offs,
     ):
 
         gain_row = held.tile([1, 2 * FEATURES], F32, name="gain_row")
-        nc.scalar.dma_start(
+        nc.sync.dma_start(
             gain_row[:].rearrange("p (r h) -> p r h", r=2),
             gain.rearrange("h o -> o h").unsqueeze(1).to_broadcast([1, 2, FEATURES]),
         )

@@ -11,6 +11,7 @@ FEATURES = 128
 HALF = FEATURES // 2
 TOKENS = 128
 SLOTS = 1024
+SQUARE = 32
 
 
 def tile_qwen3vltextattention_kernel(tc, base, kn, gain, cos_tab, sin_tab, offs, out):
@@ -30,6 +31,11 @@ def tile_qwen3vltextattention_kernel(tc, base, kn, gain, cos_tab, sin_tab, offs,
         both_keys = held.tile([FEATURES, HEADS, TOKENS], F32, name="both_keys")
         nc.sync.dma_start(both_keys[:], kn.rearrange("(a h) j -> h a j", a=HEADS))
         keys = [both_keys[:, a, :] for a in range(HEADS)]
+        gain_squares = held.tile([FEATURES, SQUARE], F32, name="gain_squares", align_bytes=64)
+        nc.vector.memset(gain_squares[:], 0.0)
+        nc.sync.dma_start(
+            gain_squares[0:FEATURES:SQUARE, :], gain.rearrange("(b i) o -> b (i o)", i=SQUARE)
+        )
         cosines = held.tile([FEATURES, TOKENS], F32, name="cosines")
         nc.sync.dma_start(cosines[:], cos_tab)
         sines = held.tile([FEATURES, TOKENS], F32, name="sines")
@@ -42,12 +48,13 @@ def tile_qwen3vltextattention_kernel(tc, base, kn, gain, cos_tab, sin_tab, offs,
             nc.sync.dma_start(window[:], base[blocks[a], :])
             windows.append(window)
 
+        flipped_squares = held.tile([FEATURES, SQUARE], F32, name="flipped_squares", align_bytes=64)
+        nc.vector.transpose(flipped_squares[:], gain_squares[:])
+        own_gain = flipped_squares[:, 0:1]
         one = held.tile([1, 1], F32, name="one")
         nc.vector.memset(one[:], 1.0)
-        gain_columns = psum.tile([FEATURES, 2], F32, name="gain_columns")
-        own_gain, partner_gain = gain_columns[:, 0:1], gain_columns[:, 1:2]
-        nc.tensor.matmul(own_gain, gain_row[:, 0:FEATURES], one[:])
-        nc.tensor.matmul(partner_gain, gain_row[:, HALF : HALF + FEATURES], one[:])
+        partner_gain = psum.tile([FEATURES, 1], F32, name="partner_gain")
+        nc.tensor.matmul(partner_gain[:], gain_row[:, HALF : HALF + FEATURES], one[:])
 
         swap = held.tile([FEATURES, FEATURES], F32, name="swap")
         nc.gpsimd.memset(swap[:], 0.0)
@@ -76,7 +83,7 @@ def tile_qwen3vltextattention_kernel(tc, base, kn, gain, cos_tab, sin_tab, offs,
         for a in range(HEADS):
             rotated = held.tile([FEATURES, TOKENS], F32, name=f"rotated{a}")
             nc.vector.scalar_tensor_tensor(
-                rotated[:], partners[a][:], partner_gain, sines[:], MULT, MULT
+                rotated[:], partners[a][:], partner_gain[:], sines[:], MULT, MULT
             )
             nc.vector.tensor_tensor(
                 windows[a][:].indirect(offsets[:]), directs[a][:], rotated[:], ADD

@@ -74,11 +74,17 @@ def tile_qwen3vltextattention_kernel(tc, base, kn, gain, cos_tab, sin_tab, offs,
             nc.tensor.matmul(partner[:], swap[:], keys[a])
             partners.append(partner)
 
-        directs = []
-        for a in range(HEADS):
-            direct = held.tile([FEATURES, TOKENS], F32, name=f"direct{a}")
-            nc.vector.scalar_tensor_tensor(direct[:], keys[a], own_gain, cosines[:], MULT, MULT)
-            directs.append(direct)
+        both_heads = [FEATURES, HEADS, TOKENS]
+        both_directs = held.tile(both_heads, F32, name="both_directs")
+        nc.vector.scalar_tensor_tensor(
+            both_directs[:],
+            both_keys[:],
+            own_gain,
+            cosines[:].unsqueeze(1).to_broadcast(both_heads),
+            MULT,
+            MULT,
+        )
+        directs = [both_directs[:, a, :] for a in range(HEADS)]
 
         for a in range(HEADS):
             rotated = held.tile([FEATURES, TOKENS], F32, name=f"rotated{a}")
@@ -86,6 +92,6 @@ def tile_qwen3vltextattention_kernel(tc, base, kn, gain, cos_tab, sin_tab, offs,
                 rotated[:], partners[a][:], partner_gain[:], sines[:], MULT, MULT
             )
             nc.vector.tensor_tensor(
-                windows[a][:].indirect(offsets[:]), directs[a][:], rotated[:], ADD
+                windows[a][:].indirect(offsets[:]), directs[a], rotated[:], ADD
             )
             nc.sync.dma_start(out[blocks[a], :], windows[a][:])

@@ -12,6 +12,7 @@ HALF = FEATURES // 2
 TOKENS = 128
 SLOTS = 1024
 SQUARE = 32
+BURST = 256
 
 
 def tile_qwen3vltextattention_kernel(tc, base, kn, gain, cos_tab, sin_tab, offs, out):
@@ -28,7 +29,7 @@ def tile_qwen3vltextattention_kernel(tc, base, kn, gain, cos_tab, sin_tab, offs,
             gain.rearrange("h o -> o h").unsqueeze(1).to_broadcast([1, 2, FEATURES]),
         )
         blocks = [slice(a * FEATURES, (a + 1) * FEATURES) for a in range(HEADS)]
-        both_keys = held.tile([FEATURES, HEADS, TOKENS], F32, name="both_keys")
+        both_keys = held.tile([FEATURES, HEADS, TOKENS], F32, name="both_keys", align_bytes=BURST)
         nc.sync.dma_start(both_keys[:], kn.rearrange("(a h) j -> h a j", a=HEADS))
         keys = [both_keys[:, a, :] for a in range(HEADS)]
         gain_squares = held.tile([FEATURES, SQUARE], F32, name="gain_squares", align_bytes=64)
@@ -36,15 +37,15 @@ def tile_qwen3vltextattention_kernel(tc, base, kn, gain, cos_tab, sin_tab, offs,
         nc.sync.dma_start(
             gain_squares[0:FEATURES:SQUARE, :], gain.rearrange("(b i) o -> b (i o)", i=SQUARE)
         )
-        cosines = held.tile([FEATURES, TOKENS], F32, name="cosines")
+        cosines = held.tile([FEATURES, TOKENS], F32, name="cosines", align_bytes=BURST)
         nc.sync.dma_start(cosines[:], cos_tab)
-        sines = held.tile([FEATURES, TOKENS], F32, name="sines")
+        sines = held.tile([FEATURES, TOKENS], F32, name="sines", align_bytes=BURST)
         nc.sync.dma_start(sines[:], sin_tab)
         offsets = held.tile([FEATURES, TOKENS // 16], U16, name="offsets")
         nc.sync.dma_start(offsets[:], offs)
         windows = []
         for a in range(HEADS):
-            window = held.tile([FEATURES, SLOTS], F32, name=f"window{a}")
+            window = held.tile([FEATURES, SLOTS], F32, name=f"window{a}", align_bytes=BURST)
             nc.sync.dma_start(window[:], base[blocks[a], :])
             windows.append(window)
 

@@ -34,7 +34,7 @@ def tile_qwen3vltextattention_kernel(tc, base, kn, gain, cos_tab, sin_tab, offs,
         keys = [both_keys[:, a, :] for a in range(HEADS)]
         gain_squares = held.tile([FEATURES, SQUARE], F32, name="gain_squares", align_bytes=64)
         nc.vector.memset(gain_squares[:], 0.0)
-        nc.sync.dma_start(
+        nc.scalar.dma_start(
             gain_squares[0:FEATURES:SQUARE, :], gain.rearrange("(b i) o -> b (i o)", i=SQUARE)
         )
         cosines = held.tile([FEATURES, TOKENS], F32, name="cosines", align_bytes=BURST)

@@ -12,6 +12,7 @@ HALF = FEATURES // 2
 TOKENS = 128
 SLOTS = 1024
 SQUARE = 32
+QUARTERS = 4
 BURST = 256
 
 
@@ -95,4 +96,6 @@ def tile_qwen3vltextattention_kernel(tc, base, kn, gain, cos_tab, sin_tab, offs,
             nc.vector.tensor_tensor(
                 windows[a][:].indirect(offsets[:]), directs[a], rotated[:], ADD
             )
-            nc.sync.dma_start(out[blocks[a], :], windows[a][:])
+            for first in range(QUARTERS):
+                rows = slice(a * FEATURES + first, (a + 1) * FEATURES, QUARTERS)
+                nc.sync.dma_start(out[rows, :], windows[a][first:FEATURES:QUARTERS, :])

@@ -11,7 +11,6 @@ FEATURES = 128
 HALF = FEATURES // 2
 TOKENS = 128
 SLOTS = 1024
-SQUARE = 32
 QUARTERS = 4
 BURST = 256
 
@@ -24,20 +23,17 @@ def tile_qwen3vltextattention_kernel(tc, base, kn, gain, cos_tab, sin_tab, offs,
         tc.psum_pool(name="psum", bufs=1) as psum,
     ):
 
-        gain_row = held.tile([1, 2 * FEATURES], F32, name="gain_row")
+        gain_halves = held.tile([2, FEATURES], F32, name="gain_halves")
         nc.sync.dma_start(
-            gain_row[:].rearrange("p (r h) -> p r h", r=2),
-            gain.rearrange("h o -> o h").unsqueeze(1).to_broadcast([1, 2, FEATURES]),
+            gain_halves[:].rearrange("r (t i) -> r t i", t=2),
+            gain.rearrange("(r i) o -> r o i", r=2).to_broadcast([2, 2, HALF]),
         )
         blocks = [slice(a * FEATURES, (a + 1) * FEATURES) for a in range(HEADS)]
-        both_keys = held.tile([FEATURES, HEADS, TOKENS], F32, name="both_keys", align_bytes=BURST)
-        nc.sync.dma_start(both_keys[:], kn.rearrange("(a h) j -> h a j", a=HEADS))
-        keys = [both_keys[:, a, :] for a in range(HEADS)]
-        gain_squares = held.tile([FEATURES, SQUARE], F32, name="gain_squares", align_bytes=64)
-        nc.vector.memset(gain_squares[:], 0.0)
-        nc.scalar.dma_start(
-            gain_squares[0:FEATURES:SQUARE, :], gain.rearrange("(b i) o -> b (i o)", i=SQUARE)
-        )
+        keys = []
+        for a in range(HEADS):
+            key = held.tile([FEATURES, TOKENS], F32, name=f"key{a}", align_bytes=BURST)
+            nc.sync.dma_start(key[:], kn[blocks[a], :])
+            keys.append(key)
         cosines = held.tile([FEATURES, TOKENS], F32, name="cosines", align_bytes=BURST)
         nc.sync.dma_start(cosines[:], cos_tab)
         sines = held.tile([FEATURES, TOKENS], F32, name="sines", align_bytes=BURST)
@@ -49,14 +45,6 @@ def tile_qwen3vltextattention_kernel(tc, base, kn, gain, cos_tab, sin_tab, offs,
             window = held.tile([FEATURES, SLOTS], F32, name=f"window{a}", align_bytes=BURST)
             nc.sync.dma_start(window[:], base[blocks[a], :])
             windows.append(window)
-
-        flipped_squares = held.tile([FEATURES, SQUARE], F32, name="flipped_squares", align_bytes=64)
-        nc.vector.transpose(flipped_squares[:], gain_squares[:])
-        own_gain = flipped_squares[:, 0:1]
-        one = held.tile([1, 1], F32, name="one")
-        nc.vector.memset(one[:], 1.0)
-        partner_gain = psum.tile([FEATURES, 1], F32, name="partner_gain")
-        nc.tensor.matmul(partner_gain[:], gain_row[:, HALF : HALF + FEATURES], one[:])
 
         swap = held.tile([FEATURES, FEATURES], F32, name="swap")
         nc.gpsimd.memset(swap[:], 0.0)
@@ -70,31 +58,33 @@ def tile_qwen3vltextattention_kernel(tc, base, kn, gain, cos_tab, sin_tab, offs,
                 base=int(sign) * HALF,
                 channel_multiplier=1,
             )
+        halves = psum.tile([FEATURES, 2], F32, name="halves")
+        nc.tensor.matmul(halves[:], gain_halves[:], swap[0:2, HALF : HALF + 2])
+        gains = held.tile([FEATURES, 2], F32, name="gains")
+        nc.vector.tensor_copy(gains[0:HALF, :], halves[0:HALF, :])
+        nc.vector.tensor_copy(gains[HALF:FEATURES, :], halves[HALF:FEATURES, ::-1])
+        own_gain, partner_gain = gains[:, 0:1], gains[:, 1:2]
         partners = []
         for a in range(HEADS):
             partner = psum.tile([FEATURES, TOKENS], F32, name=f"partner{a}")
-            nc.tensor.matmul(partner[:], swap[:], keys[a])
+            nc.tensor.matmul(partner[:], swap[:], keys[a][:])
             partners.append(partner)
 
-        both_heads = [FEATURES, HEADS, TOKENS]
-        both_directs = held.tile(both_heads, F32, name="both_directs")
-        nc.vector.scalar_tensor_tensor(
-            both_directs[:],
-            both_keys[:],
-            own_gain,
-            cosines[:].unsqueeze(1).to_broadcast(both_heads),
-            MULT,
-            MULT,
-        )
-        directs = [both_directs[:, a, :] for a in range(HEADS)]
+        directs = []
+        for a in range(HEADS):
+            direct = held.tile([FEATURES, TOKENS], F32, name=f"direct{a}")
+            nc.vector.scalar_tensor_tensor(
+                direct[:], keys[a][:], own_gain, cosines[:], MULT, MULT
+            )
+            directs.append(direct)
 
         for a in range(HEADS):
             rotated = held.tile([FEATURES, TOKENS], F32, name=f"rotated{a}")
             nc.vector.scalar_tensor_tensor(
-                rotated[:], partners[a][:], partner_gain[:], sines[:], MULT, MULT
+                rotated[:], partners[a][:], partner_gain, sines[:], MULT, MULT
             )
             nc.vector.tensor_tensor(
-                windows[a][:].indirect(offsets[:]), directs[a], rotated[:], ADD
+                windows[a][:].indirect(offsets[:]), directs[a][:], rotated[:], ADD
             )
             for first in range(QUARTERS):
                 rows = slice(a * FEATURES + first, (a + 1) * FEATURES, QUARTERS)

import concourse.mybir as mybir

F32 = mybir.dt.float32
U16 = mybir.dt.uint16
MULT = mybir.AluOpType.mult
ADD = mybir.AluOpType.add
NOT_EQUAL = mybir.AluOpType.not_equal

HEADS = 2
FEATURES = 128
HALF = FEATURES // 2
TOKENS = 128
SLOTS = 1024
QUARTERS = 4
BURST = 256


def tile_qwen3vltextattention_kernel(tc, base, kn, gain, cos_tab, sin_tab, offs, out):
    nc = tc.nc

    with (
        tc.tile_pool(name="held", bufs=1) as held,
        tc.psum_pool(name="psum", bufs=1) as psum,
    ):

        gain_halves = held.tile([2, FEATURES], F32, name="gain_halves")
        nc.sync.dma_start(
            gain_halves[:].rearrange("r (t i) -> r t i", t=2),
            gain.rearrange("(r i) o -> r o i", r=2).to_broadcast([2, 2, HALF]),
        )
        blocks = [slice(a * FEATURES, (a + 1) * FEATURES) for a in range(HEADS)]
        keys = []
        for a in range(HEADS):
            key = held.tile([FEATURES, TOKENS], F32, name=f"key{a}", align_bytes=BURST)
            nc.sync.dma_start(key[:], kn[blocks[a], :])
            keys.append(key)
        cosines = held.tile([FEATURES, TOKENS], F32, name="cosines", align_bytes=BURST)
        nc.sync.dma_start(cosines[:], cos_tab)
        sines = held.tile([FEATURES, TOKENS], F32, name="sines", align_bytes=BURST)
        nc.sync.dma_start(sines[:], sin_tab)
        offsets = held.tile([FEATURES, TOKENS // 16], U16, name="offsets")
        nc.sync.dma_start(offsets[:], offs)
        windows = []
        for a in range(HEADS):
            window = held.tile([FEATURES, SLOTS], F32, name=f"window{a}", align_bytes=BURST)
            nc.sync.dma_start(window[:], base[blocks[a], :])
            windows.append(window)

        swap = held.tile([FEATURES, FEATURES], F32, name="swap")
        nc.gpsimd.memset(swap[:], 0.0)
        for sign in (-1.0, 1.0):
            nc.gpsimd.affine_select(
                out=swap[:],
                in_=swap[:],
                pattern=[[-1, FEATURES]],
                compare_op=NOT_EQUAL,
                fill=sign,
                base=int(sign) * HALF,
                channel_multiplier=1,
            )
        halves = psum.tile([FEATURES, 2], F32, name="halves")
        nc.tensor.matmul(halves[:], gain_halves[:], swap[0:2, HALF : HALF + 2])
        gains = held.tile([FEATURES, 2], F32, name="gains")
        nc.vector.tensor_copy(gains[0:HALF, :], halves[0:HALF, :])
        nc.vector.tensor_copy(gains[HALF:FEATURES, :], halves[HALF:FEATURES, ::-1])
        own_gain, partner_gain = gains[:, 0:1], gains[:, 1:2]
        partners = []
        for a in range(HEADS):
            partner = psum.tile([FEATURES, TOKENS], F32, name=f"partner{a}")
            nc.tensor.matmul(partner[:], swap[:], keys[a][:])
            partners.append(partner)

        directs = []
        for a in range(HEADS):
            direct = held.tile([FEATURES, TOKENS], F32, name=f"direct{a}")
            nc.vector.scalar_tensor_tensor(
                direct[:], keys[a][:], own_gain, cosines[:], MULT, MULT
            )
            directs.append(direct)

        for a in range(HEADS):
            rotated = held.tile([FEATURES, TOKENS], F32, name=f"rotated{a}")
            nc.vector.scalar_tensor_tensor(
                rotated[:], partners[a][:], partner_gain, sines[:], MULT, MULT
            )
            nc.vector.tensor_tensor(
                windows[a][:].indirect(offsets[:]), directs[a][:], rotated[:], ADD
            )
            for first in range(QUARTERS):
                rows = slice(a * FEATURES + first, (a + 1) * FEATURES, QUARTERS)
                nc.sync.dma_start(out[rows, :], windows[a][first:FEATURES:QUARTERS, :])
